import numpy as np
import ml_dtypes


def mxq(x, axis, fmt="e4m3"):
    dtype, down = {"e4m3": (ml_dtypes.float8_e4m3fn, 7), "e5m2": (ml_dtypes.float8_e5m2, 14)}[fmt]
    v = np.moveaxis(np.asarray(x, np.float32).astype(ml_dtypes.bfloat16).astype(np.float64), axis, -1)
    blocks = v.reshape(v.shape[:-1] + (-1, 32))
    amax = np.abs(blocks).max(-1, keepdims=True)
    byte = np.maximum(np.where(amax > 0, np.frexp(amax)[1] - 1 + 127, 0) - down, 1)
    scale = np.exp2(byte - 127.0)
    codes = (blocks / scale).astype(np.float32).astype(dtype).astype(np.float64)
    return np.moveaxis((codes * scale).reshape(v.shape), -1, axis)


WIDE = False


def mx_kscale(k):
    if not WIDE:
        return np.ones(k)
    levels = np.array([10, -10, 5, -5, 0])
    a = np.random.permutation(np.resize(levels, k // 512 * 4)).reshape(k // 512, 4)
    idx = np.arange(k)
    return np.exp2(a[idx // 512, idx % 128 // 32])


BF16 = ml_dtypes.bfloat16


def bf(x):
    return np.asarray(x, np.float32).astype(BF16)


def f64(x):
    return np.asarray(x).astype(np.float64)


B, SEQ, FEAT, OUT, H1, H2 = 4096, 16, 16, 512, 512, 512
D = SEQ * FEAT


def setup_inputs():
    s, t = mx_kscale(H1), mx_kscale(H2)
    return {"h1": bf(np.random.standard_normal((B, H1))),
            "h2": bf(np.random.standard_normal((B, H2)) * 0.7),
            "W1": bf(np.random.standard_normal((H1, D)) / np.sqrt(D) * s[:, None]),
            "W2": bf(np.random.standard_normal((H2, H1)) / np.sqrt(H1) * t[:, None] / s[None, :]),
            "W3": bf(np.random.standard_normal((D, H2)) / np.sqrt(H2) / t[None, :])}


def reference(h1, h2, W1, W2, W3):
    h1, h2, W1, W2, W3 = f64(h1), f64(h2), f64(W1), f64(W2), f64(W3)
    m1 = np.where(h1 > 0, 1.0, 0.0)
    m2 = np.where(h2 > 0, 1.0, 0.0)
    w1_rows = W1.sum(axis=1)
    a = (mxq(m1 * w1_rows, 1, "e4m3") @ mxq(W2, 1, "e4m3").T) * m2
    row = mxq(a, 1, "e4m3") @ mxq(W3, 1, "e4m3").T
    w3_cols = W3.sum(axis=0)
    c = (mxq(m2 * w3_cols, 1, "e4m3") @ mxq(W2, 0, "e4m3")) * m1
    col = mxq(c, 1, "e4m3") @ mxq(W1, 0, "e4m3")
    return row - col

@@ -1,0 +1,276 @@
+from contextlib import ExitStack
+
+import concourse.mybir as mybir
+from concourse.masks import make_identity
+
+FLOPS = 2 * 4096 * 512 * 512 * 2 + 2 * 4096 * 512 * 256 * 2
+
+FP8X4 = mybir.dt.float8_e4m3fn_x4
+BF16 = mybir.dt.bfloat16
+F32 = mybir.dt.float32
+U32 = mybir.dt.uint32
+U8 = mybir.dt.uint8
+ALU = mybir.AluOpType
+ACT = mybir.ActivationFunctionType
+
+P = 128
+B = 4096
+H = 512
+D = 256
+NCH = B // P
+NB = 2
+NR = NCH // NB
+GROUPS = [2, 2, 4, 4, 4, 4, 4, 4, 4]
+PIN = True
+
+
+def tile_divergencefreemlp_pa_t_kernel(tc, h1, h2, W1, W2, W3, out):
+    nc = tc.nc
+    with ExitStack() as ctx:
+        const = ctx.enter_context(tc.tile_pool(name="const", bufs=1))
+        work = ctx.enter_context(tc.tile_pool(name="work", bufs=3))
+        psum_ht = ctx.enter_context(tc.psum_pool(name="psum_ht", bufs=2))
+        psum_ac = ctx.enter_context(tc.psum_pool(name="psum_ac", bufs=4))
+        psum_o = ctx.enter_context(tc.psum_pool(name="psum_o", bufs=2))
+        if PIN:
+            ctx.enter_context(tc.manual_schedule())
+
+        raw1 = const.tile([P, 4 * D], BF16, name="raw1")
+        raw3 = const.tile([P, 2 * H], BF16, name="raw3")
+        raw2 = const.tile([P, 4 * H], BF16, name="raw2")
+        nc.sync.dma_start(
+            out=raw1[:].rearrange("p (u x) -> p u x", u=2),
+            in_=W1.rearrange("(u p e) d -> p u (e d)", u=2, p=P, e=2),
+        )
+        nc.sync.dma_start(
+            out=raw3[:].rearrange("p (t i) -> p t i", t=2),
+            in_=W3.rearrange("(t p) i -> p t i", p=P),
+        )
+        hv = [h1.rearrange("(p n) j -> p n j", n=NCH), h2.rearrange("(p n) j -> p n j", n=NCH)]
+        where = {}
+        n0 = 0
+        for g, ln in enumerate(GROUPS):
+            for x in range(2):
+                hs = const.tile([P, ln * H], BF16, name="h%d_%d" % (x, g))
+                nc.sync.dma_start(
+                    out=hs[:].rearrange("p (n j) -> p n j", n=ln), in_=hv[x][:, n0 : n0 + ln, :]
+                )
+                for l in range(ln):
+                    where[(x, n0 + l)] = (hs, l)
+            n0 += ln
+            if g == 0:
+                nc.sync.dma_start(
+                    out=raw2[:].rearrange("p (u x) -> p u x", u=2),
+                    in_=W2.rearrange("(u p e) j -> p u (e j)", u=2, p=P, e=2),
+                )
+        outv = out.rearrange("(p n) d -> p n d", n=NCH)
+
+        ident = const.tile([P, P], F32, name="ident")
+        make_identity(nc, ident[:])
+        gw = const.tile([P, 6144], BF16, name="gw", align_bytes=64)
+        gww = gw[:].bitcast(F32)
+        wcodes = const.tile([P, 1536], U32, name="wcodes", align_bytes=64)
+        wscales = const.tile([P, 1536], U8, name="wscales", align_bytes=64)
+        wsum = const.tile([P, 8], F32, name="wsum")
+        junk = const.tile([P, D], F32, name="junk")
+        wc = const.tile([P, 2 * H], BF16, name="wc")
+
+        nc.gpsimd.tensor_scalar(
+            out=gw[:, 5120:6144].rearrange("p (d t) -> p d t", t=4),
+            in0=raw1[:].rearrange("p (t d) -> p d t", t=4),
+            scalar1=-1.0,
+            scalar2=0.0,
+            op0=ALU.mult,
+            op1=ALU.add,
+        )
+        for t in range(4):
+            nc.scalar.activation(
+                out=junk[:], in_=raw1[:, t * D : (t + 1) * D], func=ACT.Copy, accum_out=wsum[:, t : t + 1]
+            )
+        raw3w = raw3[:].bitcast(F32)
+        ps3 = psum_ht.tile([P, 512], F32, name="ps3", tag="ht")
+        for dh in range(2):
+            for u in range(2):
+                nc.tensor.transpose(
+                    out=ps3[:, u * 256 + dh * P : u * 256 + (dh + 1) * P],
+                    in_=raw3w[:, dh * 256 + u * P : dh * 256 + (u + 1) * P],
+                    identity=ident[:],
+                )
+        nc.scalar.copy(
+            out=gww[:, 2048:2560].rearrange("p (c u) -> p c u", u=2),
+            in_=ps3[:].rearrange("p (u c) -> p c u", u=2),
+        )
+        g3 = gw[:, 4096:5120].rearrange("p (d t) -> p t d", t=4)
+        for t in range(4):
+            nc.scalar.activation(
+                out=junk[:], in_=g3[:, t, :], func=ACT.Copy, accum_out=wsum[:, 4 + t : 5 + t]
+            )
+        nc.vector.tensor_copy(
+            out=wc[:].rearrange("p (x b t) -> p x b t", x=2, t=4),
+            in_=wsum[:].rearrange("p (x t) -> p x t", x=2).unsqueeze(2).to_broadcast([P, 2, P, 4]),
+        )
+
+        hts = {}
+        mtiles = {}
+        ups = {}
+        upcodes = {}
+        acbs = {}
+        acms = {}
+        accodes = {}
+
+        def transposes(k):
+            ht_sb = work.tile([P, 2 * NB * H], BF16, name="ht_sb", tag="ht_sb", bufs=3)
+            htw = ht_sb[:].bitcast(F32).rearrange("p (x c w) -> p x c w", x=2, c=NB)
+            banks = []
+            for c in range(NB):
+                bank = psum_ht.tile([P, 512], F32, name="ht", tag="ht")
+                for x in range(2):
+                    src, l = where[(x, k * NB + c)]
+                    srcw = src[:].bitcast(F32)
+                    for u in range(2):
+                        nc.tensor.transpose(
+                            out=bank[:, (2 * x + u) * P : (2 * x + u + 1) * P],
+                            in_=srcw[:, l * 256 + u * P : l * 256 + (u + 1) * P],
+                            identity=ident[:],
+                        )
+                banks.append(bank)
+            for c in range(NB):
+                nc.scalar.copy(
+                    out=htw[:, :, c, :].rearrange("p x (b u) -> p x b u", u=2),
+                    in_=banks[c][:].rearrange("p (x u b) -> p x b u", x=2, u=2),
+                )
+            hts[k] = ht_sb
+
+        def make_mask(k):
+            m = work.tile([P, 2 * NB * H], BF16, name="mask", tag="mask", bufs=4)
+            nc.vector.tensor_single_scalar(out=m[:], in_=hts[k][:], scalar=0.0, op=ALU.is_gt)
+            mtiles[k] = m
+
+        def make_up(k):
+            up = work.tile([P, 2 * NB * H], BF16, name="up", tag="up", bufs=2, align_bytes=64)
+            nc.vector.tensor_tensor(
+                out=up[:].rearrange("p (x c w) -> p x c w", x=2, c=NB),
+                in0=mtiles[k][:].rearrange("p (x c w) -> p x c w", x=2, c=NB),
+                in1=wc[:].rearrange("p (x w) -> p x w", x=2).unsqueeze(2).to_broadcast([P, 2, NB, H]),
+                op=ALU.mult,
+            )
+            ups[k] = up
+
+        def quantise(src, tag):
+            codes = work.tile([P, 2 * NB * P], U32, name=tag + "_c", tag=tag + "_c", bufs=3, align_bytes=64)
+            scales = work.tile([P, 2 * NB * P], U8, name=tag + "_s", tag=tag + "_s", bufs=3, align_bytes=64)
+            nc.vector.quantize_mx(out=codes[:].bitcast(FP8X4), scales=scales[:], in_=src[:])
+            return (codes, scales)
+
+        def first_matmuls(k):
+            codes, scales = upcodes[k]
+            acb = work.tile([P, 2 * NB * H], BF16, name="acb", tag="acb", bufs=3)
+            for c in range(NB):
+                for xin in range(2):
+                    xo = 1 - xin
+                    ps = psum_ac.tile([P, 512], F32, name="ac", tag="ac")
+                    lo = xin * NB * P + c * P
+                    for t in range(4):
+                        wlo = 512 * xin + t * P
+                        nc.tensor.matmul_mx(
+                            out=ps[:, t * P : (t + 1) * P],
+                            lhsT=wcodes[:, wlo : wlo + P].bitcast(FP8X4),
+                            lhsT_scale=wscales[:, wlo : wlo + P],
+                            rhs=codes[:, lo : lo + P].bitcast(FP8X4),
+                            rhs_scale=scales[:, lo : lo + P],
+                            start=True,
+                            stop=True,
+                        )
+                    olo = xo * NB * H + c * H
+                    nc.scalar.copy(
+                        out=acb[:, olo : olo + H].rearrange("p (b t) -> p b t", t=4),
+                        in_=ps[:].rearrange("p (t b) -> p b t", t=4),
+                    )
+            acbs[k] = acb
+
+        def mask_ac(k):
+            acm = work.tile([P, 2 * NB * H], BF16, name="acm", tag="acm", bufs=2, align_bytes=64)
+            nc.vector.tensor_tensor(out=acm[:], in0=acbs[k][:], in1=mtiles[k][:], op=ALU.mult)
+            acms[k] = acm
+
+        def last_matmuls(k):
+            codes, scales = accodes[k]
+            o = psum_o.tile([P, NB * D], F32, name="o", tag="o")
+            for c in range(NB):
+                alo = NB * P + c * P
+                clo = c * P
+                nc.tensor.matmul_mx(
+                    out=o[:, c * D : (c + 1) * D],
+                    lhsT=codes[:, alo : alo + P].bitcast(FP8X4),
+                    lhsT_scale=scales[:, alo : alo + P],
+                    rhs=wcodes[:, 1024:1280].bitcast(FP8X4),
+                    rhs_scale=wscales[:, 1024:1280],
+                    start=True,
+                    stop=False,
+                )
+                nc.tensor.matmul_mx(
+                    out=o[:, c * D : (c + 1) * D],
+                    lhsT=codes[:, clo : clo + P].bitcast(FP8X4),
+                    lhsT_scale=scales[:, clo : clo + P],
+                    rhs=wcodes[:, 1280:1536].bitcast(FP8X4),
+                    rhs_scale=wscales[:, 1280:1536],
+                    start=False,
+                    stop=True,
+                )
+            osb = work.tile([P, NB * D], F32, name="osb", tag="osb", bufs=3)
+            nc.scalar.copy(out=osb[:], in_=o[:])
+            nc.sync.dma_start(
+                out=outv[:, k * NB : (k + 1) * NB, :], in_=osb[:].rearrange("p (n d) -> p n d", n=NB)
+            )
+
+        transposes(0)
+
+        raw2w = raw2[:].bitcast(F32)
+        for g in range(2):
+            ps2 = psum_ht.tile([P, 512], F32, name="ps2", tag="ht")
+            for tt in range(2):
+                t = 2 * g + tt
+                for u in range(2):
+                    nc.tensor.transpose(
+                        out=ps2[:, u * 256 + tt * P : u * 256 + (tt + 1) * P],
+                        in_=raw2w[:, t * 256 + u * P : t * 256 + (u + 1) * P],
+                        identity=ident[:],
+                    )
+            nc.scalar.copy(
+                out=gww[:, g * 512 : (g + 1) * 512].rearrange("p (c u) -> p c u", u=2),
+                in_=ps2[:].rearrange("p (u c) -> p c u", u=2),
+            )
+
+        raw2v = raw2[:].rearrange("p (t u q e) -> p t u q e", t=4, u=2, q=P, e=2)
+        for i in range(NR + 3):
+            if 0 <= i - 3 < NR:
+                last_matmuls(i - 3)
+            if i + 1 < NR:
+                transposes(i + 1)
+            if 0 <= i - 1 < NR:
+                first_matmuls(i - 1)
+            if i < NR:
+                make_mask(i)
+            if 0 <= i - 2 < NR:
+                mask_ac(i - 2)
+            if i < NR:
+                make_up(i)
+            if i == 0:
+                for u in range(2):
+                    for e in range(2):
+                        lo = 2048 + (2 * u + e) * H
+                        nc.vector.tensor_copy(
+                            out=gw[:, lo : lo + H].rearrange("p (q t) -> p q t", t=4),
+                            in_=raw2v[:, :, u, :, e].rearrange("p t q -> p q t"),
+                        )
+            if 0 <= i - 2 < NR:
+                accodes[i - 2] = quantise(acms[i - 2], "ac")
+            if i < NR:
+                upcodes[i] = quantise(ups[i], "up")
+            if i == 0:
+                for s in range(3):
+                    nc.vector.quantize_mx(
+                        out=wcodes[:, s * 512 : (s + 1) * 512].bitcast(FP8X4),
+                        scales=wscales[:, s * 512 : (s + 1) * 512],
+                        in_=gw[:, s * 2048 : (s + 1) * 2048],
+                    )

@@ -12,6 +12,7 @@ U32 = mybir.dt.uint32
 U8 = mybir.dt.uint8
 ALU = mybir.AluOpType
 ACT = mybir.ActivationFunctionType
+AX = mybir.AxisListType
 
 P = 128
 B = 4096
@@ -19,13 +20,19 @@ H = 512
 D = 256
 NCH = B // P
 NB = 2
-NR = NCH // NB
+SIZES = [2] * 15 + [1, 1]
 GROUPS = [2, 2, 4, 4, 4, 4, 4, 4, 4]
+LT = 1
+LM = 1
+LA = 3
+LO = 1
 PIN = True
 
 
 def tile_divergencefreemlp_pa_t_kernel(tc, h1, h2, W1, W2, W3, out):
     nc = tc.nc
+    NR = len(SIZES)
+    starts = [sum(SIZES[:k]) for k in range(NR)]
     with ExitStack() as ctx:
         const = ctx.enter_context(tc.tile_pool(name="const", bufs=1))
         work = ctx.enter_context(tc.tile_pool(name="work", bufs=3))
@@ -39,12 +46,12 @@ def tile_divergencefreemlp_pa_t_kernel(tc, h1, h2, W1, W2, W3, out):
         raw3 = const.tile([P, 2 * H], BF16, name="raw3")
         raw2 = const.tile([P, 4 * H], BF16, name="raw2")
         nc.sync.dma_start(
-            out=raw1[:].rearrange("p (u x) -> p u x", u=2),
-            in_=W1.rearrange("(u p e) d -> p u (e d)", u=2, p=P, e=2),
-        )
-        nc.sync.dma_start(
             out=raw3[:].rearrange("p (t i) -> p t i", t=2),
             in_=W3.rearrange("(t p) i -> p t i", p=P),
+        )
+        nc.sync.dma_start(
+            out=raw1[:].rearrange("p (u x) -> p u x", u=2),
+            in_=W1.rearrange("(u p e) d -> p u (e d)", u=2, p=P, e=2),
         )
         hv = [h1.rearrange("(p n) j -> p n j", n=NCH), h2.rearrange("(p n) j -> p n j", n=NCH)]
         where = {}
@@ -72,8 +79,7 @@ def tile_divergencefreemlp_pa_t_kernel(tc, h1, h2, W1, W2, W3, out):
         wcodes = const.tile([P, 1536], U32, name="wcodes", align_bytes=64)
         wscales = const.tile([P, 1536], U8, name="wscales", align_bytes=64)
         wsum = const.tile([P, 8], F32, name="wsum")
-        junk = const.tile([P, D], F32, name="junk")
-        wc = const.tile([P, 2 * H], BF16, name="wc")
+        wc = const.tile([P, 2 * NB * H], BF16, name="wc")
 
         nc.gpsimd.tensor_scalar(
             out=gw[:, 5120:6144].rearrange("p (d t) -> p d t", t=4),
@@ -83,10 +89,9 @@ def tile_divergencefreemlp_pa_t_kernel(tc, h1, h2, W1, W2, W3, out):
             op0=ALU.mult,
             op1=ALU.add,
         )
-        for t in range(4):
-            nc.scalar.activation(
-                out=junk[:], in_=raw1[:, t * D : (t + 1) * D], func=ACT.Copy, accum_out=wsum[:, t : t + 1]
-            )
+        nc.vector.tensor_reduce(
+            out=wsum[:, 0:4], in_=raw1[:].rearrange("p (t d) -> p t d", t=4), axis=AX.X, op=ALU.add
+        )
         raw3w = raw3[:].bitcast(F32)
         ps3 = psum_ht.tile([P, 512], F32, name="ps3", tag="ht")
         for dh in range(2):
@@ -100,15 +105,15 @@ def tile_divergencefreemlp_pa_t_kernel(tc, h1, h2, W1, W2, W3, out):
             out=gww[:, 2048:2560].rearrange("p (c u) -> p c u", u=2),
             in_=ps3[:].rearrange("p (u c) -> p c u", u=2),
         )
-        g3 = gw[:, 4096:5120].rearrange("p (d t) -> p t d", t=4)
-        for t in range(4):
-            nc.scalar.activation(
-                out=junk[:], in_=g3[:, t, :], func=ACT.Copy, accum_out=wsum[:, 4 + t : 5 + t]
-            )
+        nc.vector.tensor_reduce(
+            out=wsum[:, 4:8], in_=gw[:, 4096:5120].rearrange("p (d t) -> p t d", t=4), axis=AX.X, op=ALU.add
+        )
         nc.vector.tensor_copy(
-            out=wc[:].rearrange("p (x b t) -> p x b t", x=2, t=4),
+            out=wc[:].rearrange("p (x c b t) -> p x c b t", x=2, c=NB, t=4)[:, :, 0, :, :],
             in_=wsum[:].rearrange("p (x t) -> p x t", x=2).unsqueeze(2).to_broadcast([P, 2, P, 4]),
         )
+        wcv = wc[:].rearrange("p (x c w) -> p x c w", x=2, c=NB)
+        nc.vector.tensor_copy(out=wcv[:, :, 1, :], in_=wcv[:, :, 0, :])
 
         hts = {}
         mtiles = {}
@@ -119,13 +124,14 @@ def tile_divergencefreemlp_pa_t_kernel(tc, h1, h2, W1, W2, W3, out):
         accodes = {}
 
         def transposes(k):
-            ht_sb = work.tile([P, 2 * NB * H], BF16, name="ht_sb", tag="ht_sb", bufs=3)
-            htw = ht_sb[:].bitcast(F32).rearrange("p (x c w) -> p x c w", x=2, c=NB)
+            nb = SIZES[k]
+            ht_sb = work.tile([P, 2 * nb * H], BF16, name="ht_sb", tag="ht_sb", bufs=LT + 2)
+            htw = ht_sb[:].bitcast(F32).rearrange("p (x c w) -> p x c w", x=2, c=nb)
             banks = []
-            for c in range(NB):
+            for c in range(nb):
                 bank = psum_ht.tile([P, 512], F32, name="ht", tag="ht")
                 for x in range(2):
-                    src, l = where[(x, k * NB + c)]
+                    src, l = where[(x, starts[k] + c)]
                     srcw = src[:].bitcast(F32)
                     for u in range(2):
                         nc.tensor.transpose(
@@ -134,7 +140,7 @@ def tile_divergencefreemlp_pa_t_kernel(tc, h1, h2, W1, W2, W3, out):
                             identity=ident[:],
                         )
                 banks.append(bank)
-            for c in range(NB):
+            for c in range(nb):
                 nc.scalar.copy(
                     out=htw[:, :, c, :].rearrange("p x (b u) -> p x b u", u=2),
                     in_=banks[c][:].rearrange("p (x u b) -> p x b u", x=2, u=2),
@@ -142,34 +148,36 @@ def tile_divergencefreemlp_pa_t_kernel(tc, h1, h2, W1, W2, W3, out):
             hts[k] = ht_sb
 
         def make_mask(k):
-            m = work.tile([P, 2 * NB * H], BF16, name="mask", tag="mask", bufs=4)
+            m = work.tile([P, 2 * SIZES[k] * H], BF16, name="mask", tag="mask", bufs=LA + LM + 2)
             nc.vector.tensor_single_scalar(out=m[:], in_=hts[k][:], scalar=0.0, op=ALU.is_gt)
             mtiles[k] = m
 
         def make_up(k):
-            up = work.tile([P, 2 * NB * H], BF16, name="up", tag="up", bufs=2, align_bytes=64)
+            nb = SIZES[k]
+            up = work.tile([P, 2 * nb * H], BF16, name="up", tag="up", bufs=2, align_bytes=64)
             nc.vector.tensor_tensor(
-                out=up[:].rearrange("p (x c w) -> p x c w", x=2, c=NB),
-                in0=mtiles[k][:].rearrange("p (x c w) -> p x c w", x=2, c=NB),
-                in1=wc[:].rearrange("p (x w) -> p x w", x=2).unsqueeze(2).to_broadcast([P, 2, NB, H]),
+                out=up[:].rearrange("p (x c w) -> p x c w", x=2, c=nb),
+                in0=mtiles[k][:].rearrange("p (x c w) -> p x c w", x=2, c=nb),
+                in1=wcv[:, :, 0:nb, :],
                 op=ALU.mult,
             )
             ups[k] = up
 
-        def quantise(src, tag):
-            codes = work.tile([P, 2 * NB * P], U32, name=tag + "_c", tag=tag + "_c", bufs=3, align_bytes=64)
-            scales = work.tile([P, 2 * NB * P], U8, name=tag + "_s", tag=tag + "_s", bufs=3, align_bytes=64)
+        def quantise(src, nb, tag):
+            codes = work.tile([P, 2 * nb * P], U32, name=tag + "_c", tag=tag + "_c", bufs=3, align_bytes=64)
+            scales = work.tile([P, 2 * nb * P], U8, name=tag + "_s", tag=tag + "_s", bufs=3, align_bytes=64)
             nc.vector.quantize_mx(out=codes[:].bitcast(FP8X4), scales=scales[:], in_=src[:])
             return (codes, scales)
 
         def first_matmuls(k):
+            nb = SIZES[k]
             codes, scales = upcodes[k]
-            acb = work.tile([P, 2 * NB * H], BF16, name="acb", tag="acb", bufs=3)
-            for c in range(NB):
+            acb = work.tile([P, 2 * nb * H], BF16, name="acb", tag="acb", bufs=LA + 1)
+            for c in range(nb):
                 for xin in range(2):
                     xo = 1 - xin
                     ps = psum_ac.tile([P, 512], F32, name="ac", tag="ac")
-                    lo = xin * NB * P + c * P
+                    lo = xin * nb * P + c * P
                     for t in range(4):
                         wlo = 512 * xin + t * P
                         nc.tensor.matmul_mx(
@@ -181,7 +189,7 @@ def tile_divergencefreemlp_pa_t_kernel(tc, h1, h2, W1, W2, W3, out):
                             start=True,
                             stop=True,
                         )
-                    olo = xo * NB * H + c * H
+                    olo = xo * nb * H + c * H
                     nc.scalar.copy(
                         out=acb[:, olo : olo + H].rearrange("p (b t) -> p b t", t=4),
                         in_=ps[:].rearrange("p (t b) -> p b t", t=4),
@@ -189,15 +197,16 @@ def tile_divergencefreemlp_pa_t_kernel(tc, h1, h2, W1, W2, W3, out):
             acbs[k] = acb
 
         def mask_ac(k):
-            acm = work.tile([P, 2 * NB * H], BF16, name="acm", tag="acm", bufs=2, align_bytes=64)
+            acm = work.tile([P, 2 * SIZES[k] * H], BF16, name="acm", tag="acm", bufs=2, align_bytes=64)
             nc.vector.tensor_tensor(out=acm[:], in0=acbs[k][:], in1=mtiles[k][:], op=ALU.mult)
             acms[k] = acm
 
         def last_matmuls(k):
+            nb = SIZES[k]
             codes, scales = accodes[k]
-            o = psum_o.tile([P, NB * D], F32, name="o", tag="o")
-            for c in range(NB):
-                alo = NB * P + c * P
+            o = psum_o.tile([P, nb * D], F32, name="o", tag="o")
+            for c in range(nb):
+                alo = nb * P + c * P
                 clo = c * P
                 nc.tensor.matmul_mx(
                     out=o[:, c * D : (c + 1) * D],
@@ -217,13 +226,21 @@ def tile_divergencefreemlp_pa_t_kernel(tc, h1, h2, W1, W2, W3, out):
                     start=False,
                     stop=True,
                 )
-            osb = work.tile([P, NB * D], F32, name="osb", tag="osb", bufs=3)
+            osb = work.tile([P, nb * D], F32, name="osb", tag="osb", bufs=3)
             nc.scalar.copy(out=osb[:], in_=o[:])
             nc.sync.dma_start(
-                out=outv[:, k * NB : (k + 1) * NB, :], in_=osb[:].rearrange("p (n d) -> p n d", n=NB)
+                out=outv[:, starts[k] : starts[k] + nb, :], in_=osb[:].rearrange("p (n d) -> p n d", n=nb)
+            )
+
+        def quantise_weights(s):
+            nc.vector.quantize_mx(
+                out=wcodes[:, s * 512 : (s + 1) * 512].bitcast(FP8X4),
+                scales=wscales[:, s * 512 : (s + 1) * 512],
+                in_=gw[:, s * 2048 : (s + 1) * 2048],
             )
 
         transposes(0)
+        make_mask(0)
 
         raw2w = raw2[:].bitcast(F32)
         for g in range(2):
@@ -240,37 +257,43 @@ def tile_divergencefreemlp_pa_t_kernel(tc, h1, h2, W1, W2, W3, out):
                 out=gww[:, g * 512 : (g + 1) * 512].rearrange("p (c u) -> p c u", u=2),
                 in_=ps2[:].rearrange("p (u c) -> p c u", u=2),
             )
-
         raw2v = raw2[:].rearrange("p (t u q e) -> p t u q e", t=4, u=2, q=P, e=2)
-        for i in range(NR + 3):
-            if 0 <= i - 3 < NR:
-                last_matmuls(i - 3)
-            if i + 1 < NR:
-                transposes(i + 1)
+        for u in range(2):
+            for e in range(2):
+                lo = 2048 + (2 * u + e) * H
+                nc.gpsimd.tensor_scalar(
+                    out=gw[:, lo : lo + H].rearrange("p (q t) -> p q t", t=4),
+                    in0=raw2v[:, :, u, :, e].rearrange("p t q -> p q t"),
+                    scalar1=1.0,
+                    scalar2=0.0,
+                    op0=ALU.mult,
+                    op1=ALU.add,
+                )
+        for k in range(1, LM + LT):
+            transposes(k)
+        for k in range(1, LM):
+            make_mask(k)
+
+        for i in range(NR + LA + LO):
             if 0 <= i - 1 < NR:
                 first_matmuls(i - 1)
-            if i < NR:
-                make_mask(i)
-            if 0 <= i - 2 < NR:
-                mask_ac(i - 2)
+            if 0 <= i - LA - LO < NR:
+                last_matmuls(i - LA - LO)
+            if i + LM + LT < NR:
+                transposes(i + LM + LT)
+            if 0 <= i - LA < NR:
+                mask_ac(i - LA)
             if i < NR:
                 make_up(i)
             if i == 0:
-                for u in range(2):
-                    for e in range(2):
-                        lo = 2048 + (2 * u + e) * H
-                        nc.vector.tensor_copy(
-                            out=gw[:, lo : lo + H].rearrange("p (q t) -> p q t", t=4),
-                            in_=raw2v[:, :, u, :, e].rearrange("p t q -> p q t"),
-                        )
-            if 0 <= i - 2 < NR:
-                accodes[i - 2] = quantise(acms[i - 2], "ac")
+                quantise_weights(0)
+            if 0 <= i - LA < NR:
+                accodes[i - LA] = quantise(acms[i - LA], SIZES[i - LA], "ac")
             if i < NR:
-                upcodes[i] = quantise(ups[i], "up")
+                upcodes[i] = quantise(ups[i], SIZES[i], "up")
             if i == 0:
-                for s in range(3):
-                    nc.vector.quantize_mx(
-                        out=wcodes[:, s * 512 : (s + 1) * 512].bitcast(FP8X4),
-                        scales=wscales[:, s * 512 : (s + 1) * 512],
-                        in_=gw[:, s * 2048 : (s + 1) * 2048],
-                    )
+                quantise_weights(1)
+            if i + LM < NR:
+                make_mask(i + LM)
+            if i == 0:
+                quantise_weights(2)

@@ -36,9 +36,7 @@ def tile_divergencefreemlp_pa_t_kernel(tc, h1, h2, W1, W2, W3, out):
     with ExitStack() as ctx:
         const = ctx.enter_context(tc.tile_pool(name="const", bufs=1))
         work = ctx.enter_context(tc.tile_pool(name="work", bufs=3))
-        psum_ht = ctx.enter_context(tc.psum_pool(name="psum_ht", bufs=2))
-        psum_ac = ctx.enter_context(tc.psum_pool(name="psum_ac", bufs=4))
-        psum_o = ctx.enter_context(tc.psum_pool(name="psum_o", bufs=2))
+        psum = ctx.enter_context(tc.psum_pool(name="psum", bufs=8))
         if PIN:
             ctx.enter_context(tc.manual_schedule())
 
@@ -93,7 +91,7 @@ def tile_divergencefreemlp_pa_t_kernel(tc, h1, h2, W1, W2, W3, out):
             out=wsum[:, 0:4], in_=raw1[:].rearrange("p (t d) -> p t d", t=4), axis=AX.X, op=ALU.add
         )
         raw3w = raw3[:].bitcast(F32)
-        ps3 = psum_ht.tile([P, 512], F32, name="ps3", tag="ht")
+        ps3 = psum.tile([P, 512], F32, name="ps3", tag="bank")
         for dh in range(2):
             for u in range(2):
                 nc.tensor.transpose(
@@ -129,7 +127,7 @@ def tile_divergencefreemlp_pa_t_kernel(tc, h1, h2, W1, W2, W3, out):
             htw = ht_sb[:].bitcast(F32).rearrange("p (x c w) -> p x c w", x=2, c=nb)
             banks = []
             for c in range(nb):
-                bank = psum_ht.tile([P, 512], F32, name="ht", tag="ht")
+                bank = psum.tile([P, 512], F32, name="ht", tag="bank")
                 for x in range(2):
                     src, l = where[(x, starts[k] + c)]
                     srcw = src[:].bitcast(F32)
@@ -176,7 +174,7 @@ def tile_divergencefreemlp_pa_t_kernel(tc, h1, h2, W1, W2, W3, out):
             for c in range(nb):
                 for xin in range(2):
                     xo = 1 - xin
-                    ps = psum_ac.tile([P, 512], F32, name="ac", tag="ac")
+                    ps = psum.tile([P, 512], F32, name="ac", tag="bank")
                     lo = xin * nb * P + c * P
                     for t in range(4):
                         wlo = 512 * xin + t * P
@@ -204,7 +202,7 @@ def tile_divergencefreemlp_pa_t_kernel(tc, h1, h2, W1, W2, W3, out):
         def last_matmuls(k):
             nb = SIZES[k]
             codes, scales = accodes[k]
-            o = psum_o.tile([P, nb * D], F32, name="o", tag="o")
+            o = psum.tile([P, nb * D], F32, name="o", tag="bank")
             for c in range(nb):
                 alo = nb * P + c * P
                 clo = c * P
@@ -244,7 +242,7 @@ def tile_divergencefreemlp_pa_t_kernel(tc, h1, h2, W1, W2, W3, out):
 
         raw2w = raw2[:].bitcast(F32)
         for g in range(2):
-            ps2 = psum_ht.tile([P, 512], F32, name="ps2", tag="ht")
+            ps2 = psum.tile([P, 512], F32, name="ps2", tag="bank")
             for tt in range(2):
                 t = 2 * g + tt
                 for u in range(2):

@@ -19,8 +19,8 @@ B = 4096
 H = 512
 D = 256
 NCH = B // P
-NB = 2
-SIZES = [2] * 15 + [1, 1]
+NB = 4
+SIZES = [2, 2, 4, 4, 4, 4, 4, 4, 2, 1, 1]
 GROUPS = [2, 2, 4, 4, 4, 4, 4, 4, 4]
 LT = 1
 LM = 1
@@ -77,7 +77,7 @@ def tile_divergencefreemlp_pa_t_kernel(tc, h1, h2, W1, W2, W3, out):
         wcodes = const.tile([P, 1536], U32, name="wcodes", align_bytes=64)
         wscales = const.tile([P, 1536], U8, name="wscales", align_bytes=64)
         wsum = const.tile([P, 8], F32, name="wsum")
-        wc = const.tile([P, 2 * NB * H], BF16, name="wc")
+        wc = const.tile([P, 2 * H], BF16, name="wc")
 
         nc.gpsimd.tensor_scalar(
             out=gw[:, 5120:6144].rearrange("p (d t) -> p d t", t=4),
@@ -107,11 +107,10 @@ def tile_divergencefreemlp_pa_t_kernel(tc, h1, h2, W1, W2, W3, out):
             out=wsum[:, 4:8], in_=gw[:, 4096:5120].rearrange("p (d t) -> p t d", t=4), axis=AX.X, op=ALU.add
         )
         nc.vector.tensor_copy(
-            out=wc[:].rearrange("p (x c b t) -> p x c b t", x=2, c=NB, t=4)[:, :, 0, :, :],
+            out=wc[:].rearrange("p (x b t) -> p x b t", x=2, t=4),
             in_=wsum[:].rearrange("p (x t) -> p x t", x=2).unsqueeze(2).to_broadcast([P, 2, P, 4]),
         )
-        wcv = wc[:].rearrange("p (x c w) -> p x c w", x=2, c=NB)
-        nc.vector.tensor_copy(out=wcv[:, :, 1, :], in_=wcv[:, :, 0, :])
+        wcv = wc[:].rearrange("p (x w) -> p x w", x=2).unsqueeze(2)
 
         hts = {}
         mtiles = {}
@@ -123,7 +122,7 @@ def tile_divergencefreemlp_pa_t_kernel(tc, h1, h2, W1, W2, W3, out):
 
         def transposes(k):
             nb = SIZES[k]
-            ht_sb = work.tile([P, 2 * nb * H], BF16, name="ht_sb", tag="ht_sb", bufs=LT + 2)
+            ht_sb = work.tile([P, 2 * nb * H], BF16, name="ht_sb", tag="ht_sb", bufs=2)
             htw = ht_sb[:].bitcast(F32).rearrange("p (x c w) -> p x c w", x=2, c=nb)
             banks = []
             for c in range(nb):
@@ -146,7 +145,7 @@ def tile_divergencefreemlp_pa_t_kernel(tc, h1, h2, W1, W2, W3, out):
             hts[k] = ht_sb
 
         def make_mask(k):
-            m = work.tile([P, 2 * SIZES[k] * H], BF16, name="mask", tag="mask", bufs=LA + LM + 2)
+            m = work.tile([P, 2 * SIZES[k] * H], BF16, name="mask", tag="mask", bufs=LA + LM)
             nc.vector.tensor_single_scalar(out=m[:], in_=hts[k][:], scalar=0.0, op=ALU.is_gt)
             mtiles[k] = m
 
@@ -156,21 +155,21 @@ def tile_divergencefreemlp_pa_t_kernel(tc, h1, h2, W1, W2, W3, out):
             nc.vector.tensor_tensor(
                 out=up[:].rearrange("p (x c w) -> p x c w", x=2, c=nb),
                 in0=mtiles[k][:].rearrange("p (x c w) -> p x c w", x=2, c=nb),
-                in1=wcv[:, :, 0:nb, :],
+                in1=wcv.to_broadcast([P, 2, nb, H]),
                 op=ALU.mult,
             )
             ups[k] = up
 
         def quantise(src, nb, tag):
-            codes = work.tile([P, 2 * nb * P], U32, name=tag + "_c", tag=tag + "_c", bufs=3, align_bytes=64)
-            scales = work.tile([P, 2 * nb * P], U8, name=tag + "_s", tag=tag + "_s", bufs=3, align_bytes=64)
+            codes = work.tile([P, 2 * nb * P], U32, name=tag + "_c", tag=tag + "_c", bufs=2, align_bytes=64)
+            scales = work.tile([P, 2 * nb * P], U8, name=tag + "_s", tag=tag + "_s", bufs=2, align_bytes=64)
             nc.vector.quantize_mx(out=codes[:].bitcast(FP8X4), scales=scales[:], in_=src[:])
             return (codes, scales)
 
         def first_matmuls(k):
             nb = SIZES[k]
             codes, scales = upcodes[k]
-            acb = work.tile([P, 2 * nb * H], BF16, name="acb", tag="acb", bufs=LA + 1)
+            acb = work.tile([P, 2 * nb * H], BF16, name="acb", tag="acb", bufs=LA, align_bytes=64)
             for c in range(nb):
                 for xin in range(2):
                     xo = 1 - xin
@@ -195,37 +194,39 @@ def tile_divergencefreemlp_pa_t_kernel(tc, h1, h2, W1, W2, W3, out):
             acbs[k] = acb
 
         def mask_ac(k):
-            acm = work.tile([P, 2 * SIZES[k] * H], BF16, name="acm", tag="acm", bufs=2, align_bytes=64)
-            nc.vector.tensor_tensor(out=acm[:], in0=acbs[k][:], in1=mtiles[k][:], op=ALU.mult)
-            acms[k] = acm
+            nc.vector.tensor_tensor(out=acbs[k][:], in0=acbs[k][:], in1=mtiles[k][:], op=ALU.mult)
+            acms[k] = acbs[k]
 
         def last_matmuls(k):
             nb = SIZES[k]
             codes, scales = accodes[k]
-            o = psum.tile([P, nb * D], F32, name="o", tag="bank")
-            for c in range(nb):
-                alo = nb * P + c * P
-                clo = c * P
-                nc.tensor.matmul_mx(
-                    out=o[:, c * D : (c + 1) * D],
-                    lhsT=codes[:, alo : alo + P].bitcast(FP8X4),
-                    lhsT_scale=scales[:, alo : alo + P],
-                    rhs=wcodes[:, 1024:1280].bitcast(FP8X4),
-                    rhs_scale=wscales[:, 1024:1280],
-                    start=True,
-                    stop=False,
-                )
-                nc.tensor.matmul_mx(
-                    out=o[:, c * D : (c + 1) * D],
-                    lhsT=codes[:, clo : clo + P].bitcast(FP8X4),
-                    lhsT_scale=scales[:, clo : clo + P],
-                    rhs=wcodes[:, 1280:1536].bitcast(FP8X4),
-                    rhs_scale=wscales[:, 1280:1536],
-                    start=False,
-                    stop=True,
-                )
-            osb = work.tile([P, nb * D], F32, name="osb", tag="osb", bufs=3)
-            nc.scalar.copy(out=osb[:], in_=o[:])
+            osb = work.tile([P, nb * D], F32, name="osb", tag="osb", bufs=2)
+            for c0 in range(0, nb, 2):
+                cn = min(2, nb - c0)
+                o = psum.tile([P, cn * D], F32, name="o", tag="bank")
+                for c in range(c0, c0 + cn):
+                    alo = nb * P + c * P
+                    clo = c * P
+                    ocols = o[:, (c - c0) * D : (c - c0 + 1) * D]
+                    nc.tensor.matmul_mx(
+                        out=ocols,
+                        lhsT=codes[:, alo : alo + P].bitcast(FP8X4),
+                        lhsT_scale=scales[:, alo : alo + P],
+                        rhs=wcodes[:, 1024:1280].bitcast(FP8X4),
+                        rhs_scale=wscales[:, 1024:1280],
+                        start=True,
+                        stop=False,
+                    )
+                    nc.tensor.matmul_mx(
+                        out=ocols,
+                        lhsT=codes[:, clo : clo + P].bitcast(FP8X4),
+                        lhsT_scale=scales[:, clo : clo + P],
+                        rhs=wcodes[:, 1280:1536].bitcast(FP8X4),
+                        rhs_scale=wscales[:, 1280:1536],
+                        start=False,
+                        stop=True,
+                    )
+                nc.scalar.copy(out=osb[:, c0 * D : (c0 + cn) * D], in_=o[:])
             nc.sync.dma_start(
                 out=outv[:, starts[k] : starts[k] + nb, :], in_=osb[:].rearrange("p (n d) -> p n d", n=nb)
             )

from contextlib import ExitStack

import concourse.mybir as mybir
from concourse.masks import make_identity

FLOPS = 2 * 4096 * 512 * 512 * 2 + 2 * 4096 * 512 * 256 * 2

FP8X4 = mybir.dt.float8_e4m3fn_x4
BF16 = mybir.dt.bfloat16
F32 = mybir.dt.float32
U32 = mybir.dt.uint32
U8 = mybir.dt.uint8
ALU = mybir.AluOpType
ACT = mybir.ActivationFunctionType
AX = mybir.AxisListType

P = 128
B = 4096
H = 512
D = 256
NCH = B // P
NB = 4
SIZES = [2, 2, 4, 4, 4, 4, 4, 4, 2, 1, 1]
GROUPS = [2, 2, 4, 4, 4, 4, 4, 4, 4]
LT = 1
LM = 1
LA = 3
LO = 1
PIN = True


def tile_divergencefreemlp_pa_t_kernel(tc, h1, h2, W1, W2, W3, out):
    nc = tc.nc
    NR = len(SIZES)
    starts = [sum(SIZES[:k]) for k in range(NR)]
    with ExitStack() as ctx:
        const = ctx.enter_context(tc.tile_pool(name="const", bufs=1))
        work = ctx.enter_context(tc.tile_pool(name="work", bufs=3))
        psum = ctx.enter_context(tc.psum_pool(name="psum", bufs=8))
        if PIN:
            ctx.enter_context(tc.manual_schedule())

        raw1 = const.tile([P, 4 * D], BF16, name="raw1")
        raw3 = const.tile([P, 2 * H], BF16, name="raw3")
        raw2 = const.tile([P, 4 * H], BF16, name="raw2")
        nc.sync.dma_start(
            out=raw3[:].rearrange("p (t i) -> p t i", t=2),
            in_=W3.rearrange("(t p) i -> p t i", p=P),
        )
        nc.sync.dma_start(
            out=raw1[:].rearrange("p (u x) -> p u x", u=2),
            in_=W1.rearrange("(u p e) d -> p u (e d)", u=2, p=P, e=2),
        )
        hv = [h1.rearrange("(p n) j -> p n j", n=NCH), h2.rearrange("(p n) j -> p n j", n=NCH)]
        where = {}
        n0 = 0
        for g, ln in enumerate(GROUPS):
            for x in range(2):
                hs = const.tile([P, ln * H], BF16, name="h%d_%d" % (x, g))
                nc.sync.dma_start(
                    out=hs[:].rearrange("p (n j) -> p n j", n=ln), in_=hv[x][:, n0 : n0 + ln, :]
                )
                for l in range(ln):
                    where[(x, n0 + l)] = (hs, l)
            n0 += ln
            if g == 0:
                nc.sync.dma_start(
                    out=raw2[:].rearrange("p (u x) -> p u x", u=2),
                    in_=W2.rearrange("(u p e) j -> p u (e j)", u=2, p=P, e=2),
                )
        outv = out.rearrange("(p n) d -> p n d", n=NCH)

        ident = const.tile([P, P], F32, name="ident")
        make_identity(nc, ident[:])
        gw = const.tile([P, 6144], BF16, name="gw", align_bytes=64)
        gww = gw[:].bitcast(F32)
        wcodes = const.tile([P, 1536], U32, name="wcodes", align_bytes=64)
        wscales = const.tile([P, 1536], U8, name="wscales", align_bytes=64)
        wsum = const.tile([P, 8], F32, name="wsum")
        wc = const.tile([P, 2 * H], BF16, name="wc")

        nc.gpsimd.tensor_scalar(
            out=gw[:, 5120:6144].rearrange("p (d t) -> p d t", t=4),
            in0=raw1[:].rearrange("p (t d) -> p d t", t=4),
            scalar1=-1.0,
            scalar2=0.0,
            op0=ALU.mult,
            op1=ALU.add,
        )
        nc.vector.tensor_reduce(
            out=wsum[:, 0:4], in_=raw1[:].rearrange("p (t d) -> p t d", t=4), axis=AX.X, op=ALU.add
        )
        raw3w = raw3[:].bitcast(F32)
        ps3 = psum.tile([P, 512], F32, name="ps3", tag="bank")
        for dh in range(2):
            for u in range(2):
                nc.tensor.transpose(
                    out=ps3[:, u * 256 + dh * P : u * 256 + (dh + 1) * P],
                    in_=raw3w[:, dh * 256 + u * P : dh * 256 + (u + 1) * P],
                    identity=ident[:],
                )
        nc.scalar.copy(
            out=gww[:, 2048:2560].rearrange("p (c u) -> p c u", u=2),
            in_=ps3[:].rearrange("p (u c) -> p c u", u=2),
        )
        nc.vector.tensor_reduce(
            out=wsum[:, 4:8], in_=gw[:, 4096:5120].rearrange("p (d t) -> p t d", t=4), axis=AX.X, op=ALU.add
        )
        nc.vector.tensor_copy(
            out=wc[:].rearrange("p (x b t) -> p x b t", x=2, t=4),
            in_=wsum[:].rearrange("p (x t) -> p x t", x=2).unsqueeze(2).to_broadcast([P, 2, P, 4]),
        )
        wcv = wc[:].rearrange("p (x w) -> p x w", x=2).unsqueeze(2)

        hts = {}
        mtiles = {}
        ups = {}
        upcodes = {}
        acbs = {}
        acms = {}
        accodes = {}

        def transposes(k):
            nb = SIZES[k]
            ht_sb = work.tile([P, 2 * nb * H], BF16, name="ht_sb", tag="ht_sb", bufs=2)
            htw = ht_sb[:].bitcast(F32).rearrange("p (x c w) -> p x c w", x=2, c=nb)
            banks = []
            for c in range(nb):
                bank = psum.tile([P, 512], F32, name="ht", tag="bank")
                for x in range(2):
                    src, l = where[(x, starts[k] + c)]
                    srcw = src[:].bitcast(F32)
                    for u in range(2):
                        nc.tensor.transpose(
                            out=bank[:, (2 * x + u) * P : (2 * x + u + 1) * P],
                            in_=srcw[:, l * 256 + u * P : l * 256 + (u + 1) * P],
                            identity=ident[:],
                        )
                banks.append(bank)
            for c in range(nb):
                nc.scalar.copy(
                    out=htw[:, :, c, :].rearrange("p x (b u) -> p x b u", u=2),
                    in_=banks[c][:].rearrange("p (x u b) -> p x b u", x=2, u=2),
                )
            hts[k] = ht_sb

        def make_mask(k):
            m = work.tile([P, 2 * SIZES[k] * H], BF16, name="mask", tag="mask", bufs=LA + LM)
            nc.vector.tensor_single_scalar(out=m[:], in_=hts[k][:], scalar=0.0, op=ALU.is_gt)
            mtiles[k] = m

        def make_up(k):
            nb = SIZES[k]
            up = work.tile([P, 2 * nb * H], BF16, name="up", tag="up", bufs=2, align_bytes=64)
            nc.vector.tensor_tensor(
                out=up[:].rearrange("p (x c w) -> p x c w", x=2, c=nb),
                in0=mtiles[k][:].rearrange("p (x c w) -> p x c w", x=2, c=nb),
                in1=wcv.to_broadcast([P, 2, nb, H]),
                op=ALU.mult,
            )
            ups[k] = up

        def quantise(src, nb, tag):
            codes = work.tile([P, 2 * nb * P], U32, name=tag + "_c", tag=tag + "_c", bufs=2, align_bytes=64)
            scales = work.tile([P, 2 * nb * P], U8, name=tag + "_s", tag=tag + "_s", bufs=2, align_bytes=64)
            nc.vector.quantize_mx(out=codes[:].bitcast(FP8X4), scales=scales[:], in_=src[:])
            return (codes, scales)

        def first_matmuls(k):
            nb = SIZES[k]
            codes, scales = upcodes[k]
            acb = work.tile([P, 2 * nb * H], BF16, name="acb", tag="acb", bufs=LA, align_bytes=64)
            for c in range(nb):
                for xin in range(2):
                    xo = 1 - xin
                    ps = psum.tile([P, 512], F32, name="ac", tag="bank")
                    lo = xin * nb * P + c * P
                    for t in range(4):
                        wlo = 512 * xin + t * P
                        nc.tensor.matmul_mx(
                            out=ps[:, t * P : (t + 1) * P],
                            lhsT=wcodes[:, wlo : wlo + P].bitcast(FP8X4),
                            lhsT_scale=wscales[:, wlo : wlo + P],
                            rhs=codes[:, lo : lo + P].bitcast(FP8X4),
                            rhs_scale=scales[:, lo : lo + P],
                            start=True,
                            stop=True,
                        )
                    olo = xo * nb * H + c * H
                    nc.scalar.copy(
                        out=acb[:, olo : olo + H].rearrange("p (b t) -> p b t", t=4),
                        in_=ps[:].rearrange("p (t b) -> p b t", t=4),
                    )
            acbs[k] = acb

        def mask_ac(k):
            nc.vector.tensor_tensor(out=acbs[k][:], in0=acbs[k][:], in1=mtiles[k][:], op=ALU.mult)
            acms[k] = acbs[k]

        def last_matmuls(k):
            nb = SIZES[k]
            codes, scales = accodes[k]
            osb = work.tile([P, nb * D], F32, name="osb", tag="osb", bufs=2)
            for c0 in range(0, nb, 2):
                cn = min(2, nb - c0)
                o = psum.tile([P, cn * D], F32, name="o", tag="bank")
                for c in range(c0, c0 + cn):
                    alo = nb * P + c * P
                    clo = c * P
                    ocols = o[:, (c - c0) * D : (c - c0 + 1) * D]
                    nc.tensor.matmul_mx(
                        out=ocols,
                        lhsT=codes[:, alo : alo + P].bitcast(FP8X4),
                        lhsT_scale=scales[:, alo : alo + P],
                        rhs=wcodes[:, 1024:1280].bitcast(FP8X4),
                        rhs_scale=wscales[:, 1024:1280],
                        start=True,
                        stop=False,
                    )
                    nc.tensor.matmul_mx(
                        out=ocols,
                        lhsT=codes[:, clo : clo + P].bitcast(FP8X4),
                        lhsT_scale=scales[:, clo : clo + P],
                        rhs=wcodes[:, 1280:1536].bitcast(FP8X4),
                        rhs_scale=wscales[:, 1280:1536],
                        start=False,
                        stop=True,
                    )
                nc.scalar.copy(out=osb[:, c0 * D : (c0 + cn) * D], in_=o[:])
            nc.sync.dma_start(
                out=outv[:, starts[k] : starts[k] + nb, :], in_=osb[:].rearrange("p (n d) -> p n d", n=nb)
            )

        def quantise_weights(s):
            nc.vector.quantize_mx(
                out=wcodes[:, s * 512 : (s + 1) * 512].bitcast(FP8X4),
                scales=wscales[:, s * 512 : (s + 1) * 512],
                in_=gw[:, s * 2048 : (s + 1) * 2048],
            )

        transposes(0)
        make_mask(0)

        raw2w = raw2[:].bitcast(F32)
        for g in range(2):
            ps2 = psum.tile([P, 512], F32, name="ps2", tag="bank")
            for tt in range(2):
                t = 2 * g + tt
                for u in range(2):
                    nc.tensor.transpose(
                        out=ps2[:, u * 256 + tt * P : u * 256 + (tt + 1) * P],
                        in_=raw2w[:, t * 256 + u * P : t * 256 + (u + 1) * P],
                        identity=ident[:],
                    )
            nc.scalar.copy(
                out=gww[:, g * 512 : (g + 1) * 512].rearrange("p (c u) -> p c u", u=2),
                in_=ps2[:].rearrange("p (u c) -> p c u", u=2),
            )
        raw2v = raw2[:].rearrange("p (t u q e) -> p t u q e", t=4, u=2, q=P, e=2)
        for u in range(2):
            for e in range(2):
                lo = 2048 + (2 * u + e) * H
                nc.gpsimd.tensor_scalar(
                    out=gw[:, lo : lo + H].rearrange("p (q t) -> p q t", t=4),
                    in0=raw2v[:, :, u, :, e].rearrange("p t q -> p q t"),
                    scalar1=1.0,
                    scalar2=0.0,
                    op0=ALU.mult,
                    op1=ALU.add,
                )
        for k in range(1, LM + LT):
            transposes(k)
        for k in range(1, LM):
            make_mask(k)

        for i in range(NR + LA + LO):
            if 0 <= i - 1 < NR:
                first_matmuls(i - 1)
            if 0 <= i - LA - LO < NR:
                last_matmuls(i - LA - LO)
            if i + LM + LT < NR:
                transposes(i + LM + LT)
            if 0 <= i - LA < NR:
                mask_ac(i - LA)
            if i < NR:
                make_up(i)
            if i == 0:
                quantise_weights(0)
            if 0 <= i - LA < NR:
                accodes[i - LA] = quantise(acms[i - LA], SIZES[i - LA], "ac")
            if i < NR:
                upcodes[i] = quantise(ups[i], SIZES[i], "up")
            if i == 0:
                quantise_weights(1)
            if i + LM < NR:
                make_mask(i + LM)
            if i == 0:
                quantise_weights(2)
